import numpy as np
import ml_dtypes

BF16 = ml_dtypes.bfloat16


def bf(x):
    return np.asarray(x, np.float32).astype(BF16)


def f32(x):
    return np.asarray(x, np.float32)


def f64(x):
    return np.asarray(x).astype(np.float64)


def striped(idx):
    return np.tile(idx.reshape(-1, 16).T, (8, 1))


C, E, T, K, S, N, KD, Q, H, R = 256, 128, 128, 4, 1024, 4096, 512, 384, 512, 8


def setup_inputs():
    return {
        "features": f32(np.random.standard_normal((C, S))),
        "edge_feats": bf(np.random.standard_normal((E, N))),
        "time_feats": bf(np.random.standard_normal((T, N))),
        "wk": bf(np.random.standard_normal((K * KD, Q)) / np.sqrt(K * KD)),
        "bk": f32(0.1 * np.random.standard_normal((Q, 1))),
        "wv": bf(np.random.standard_normal((K * KD, Q)) / np.sqrt(K * KD)),
        "bv": f32(0.1 * np.random.standard_normal((Q, 1))),
        "offs": striped(np.concatenate([np.random.permutation(S)[:H] for _ in range(R)])),
    }


def reference(features, edge_feats, time_feats, wk, bk, wv, bv, offs):
    idx = offs[:16].T.reshape(-1)
    neigh = f64(features)[:, idx]
    cat = np.concatenate([neigh, f64(edge_feats), f64(time_feats)], axis=0)
    agg = cat.reshape(KD, K, S).transpose(1, 0, 2).reshape(K * KD, S)
    key = f64(wk).T @ agg + f64(bk)
    val = f64(wv).T @ agg + f64(bv)
    return np.concatenate([key, val], axis=0)

@@ -1,0 +1,109 @@
+import concourse.mybir as mybir
+from concourse.masks import make_identity
+
+F32 = mybir.dt.float32
+BF16 = mybir.dt.bfloat16
+U16 = mybir.dt.uint16
+COPY = mybir.ActivationFunctionType.Copy
+
+P = 128
+NODES = 1024
+SLOTS = 4
+HALF = 512
+HALVES = NODES // HALF
+TABLE_BLOCKS = 2
+SLOT_BLOCKS = 4
+K_BLOCKS = SLOTS * SLOT_BLOCKS
+Q = 384
+OUT_BLOCKS = 2 * Q // P
+
+FLOPS = 2 * (2 * Q) * (K_BLOCKS * P) * NODES
+
+
+def tile_tgnlayergraphattentionembedding_kernel(
+    tc, features, edge_feats, time_feats, wk, bk, wv, bv, offs, out
+):
+    nc = tc.nc
+    with (
+        tc.tile_pool(name="held", bufs=1) as held,
+        tc.tile_pool(name="ring", bufs=4) as ring,
+        tc.psum_pool(name="psum", bufs=8) as psum,
+    ):
+        offsets = held.tile([P, SLOTS * NODES // 16], U16, name="offsets")
+        table = [held.tile([P, NODES], F32, name=f"table{b}") for b in range(TABLE_BLOCKS)]
+        weights = [held.tile([P, 2 * Q], BF16, name=f"weights{kb}") for kb in range(K_BLOCKS)]
+        agg = [
+            [held.tile([P, HALF], BF16, name=f"agg{kb}_{h}") for h in range(HALVES)]
+            for kb in range(K_BLOCKS)
+        ]
+
+        given = {2: edge_feats, 3: time_feats}
+        given_blocks = [kb for kb in range(K_BLOCKS) if kb % SLOT_BLOCKS in given]
+        neigh_blocks = [kb for kb in range(K_BLOCKS) if kb % SLOT_BLOCKS not in given]
+        k_order = given_blocks + neigh_blocks
+
+        bias_rows = held.tile([OUT_BLOCKS, P], F32, name="bias_rows")
+        nc.scalar.dma_start(bias_rows[0:3, :], bk.rearrange("(j p) o -> j (p o)", p=P))
+        nc.scalar.dma_start(bias_rows[3:6, :], bv.rearrange("(j p) o -> j (p o)", p=P))
+        identity = held.tile([OUT_BLOCKS, OUT_BLOCKS], F32, name="identity")
+        make_identity(nc, identity[:])
+        bias_bank = psum.tile([P, HALF], F32, name="bias_bank", tag="bank")
+        nc.tensor.matmul(bias_bank[:, 0:OUT_BLOCKS], bias_rows[:], identity[:], start=True, stop=True)
+        bias = held.tile([P, OUT_BLOCKS], F32, name="bias")
+        nc.vector.tensor_copy(bias[:], bias_bank[:, 0:OUT_BLOCKS])
+
+        def load_given(kb, h):
+            slot, kind = divmod(kb, SLOT_BLOCKS)
+            first = slot * NODES + h * HALF
+            nc.sync.dma_start(agg[kb][h][:], given[kind][:, first : first + HALF])
+
+        for place, kb in enumerate(k_order):
+            nc.sync.dma_start(weights[kb][:, 0:Q], wk[kb * P : (kb + 1) * P, :])
+            nc.sync.dma_start(weights[kb][:, Q : 2 * Q], wv[kb * P : (kb + 1) * P, :])
+            if kb in given_blocks:
+                load_given(kb, 0)
+            if place == 2:
+                nc.sync.dma_start(offsets[:], offs)
+                for b in range(TABLE_BLOCKS):
+                    nc.sync.dma_start(table[b][:], features[b * P : (b + 1) * P, :])
+        for kb in given_blocks:
+            load_given(kb, 1)
+
+        for h in range(HALVES):
+            for slot in range(SLOTS):
+                first = (slot * NODES + h * HALF) // 16
+                piece = offsets[:, first : first + HALF // 16]
+                for b in range(TABLE_BLOCKS):
+                    picked = ring.tile([P, HALF], F32, name="picked")
+                    nc.scalar.activation(picked[:], table[b][:].indirect(piece), COPY)
+                    nc.vector.tensor_copy(agg[slot * SLOT_BLOCKS + b][h][:], picked[:])
+
+        def finish(bank, j, h):
+            staged = ring.tile([P, HALF], F32, name="staged")
+            nc.vector.tensor_scalar_add(staged[:], bank[:], bias[:, j : j + 1])
+            nc.sync.dma_start(out[j * P : (j + 1) * P, h * HALF : (h + 1) * HALF], staged[:])
+
+        banks = [psum.tile([P, HALF], F32, name=f"bank{j}", tag="bank") for j in range(OUT_BLOCKS)]
+        for place, kb in enumerate(k_order):
+            for j in range(OUT_BLOCKS):
+                nc.tensor.matmul(
+                    banks[j][:],
+                    weights[kb][:, j * P : (j + 1) * P],
+                    agg[kb][0][:],
+                    start=place == 0,
+                    stop=place == K_BLOCKS - 1,
+                )
+        for j in range(OUT_BLOCKS):
+            finish(banks[j], j, 0)
+
+        for j in range(OUT_BLOCKS):
+            bank = psum.tile([P, HALF], F32, name="bank", tag="bank")
+            for place, kb in enumerate(k_order):
+                nc.tensor.matmul(
+                    bank[:],
+                    weights[kb][:, j * P : (j + 1) * P],
+                    agg[kb][1][:],
+                    start=place == 0,
+                    stop=place == K_BLOCKS - 1,
+                )
+            finish(bank, j, 1)

@@ -1,5 +1,4 @@
 import concourse.mybir as mybir
-from concourse.masks import make_identity
 
 F32 = mybir.dt.float32
 BF16 = mybir.dt.bfloat16
@@ -42,16 +41,6 @@ def tile_tgnlayergraphattentionembedding_kernel(
         neigh_blocks = [kb for kb in range(K_BLOCKS) if kb % SLOT_BLOCKS not in given]
         k_order = given_blocks + neigh_blocks
 
-        bias_rows = held.tile([OUT_BLOCKS, P], F32, name="bias_rows")
-        nc.scalar.dma_start(bias_rows[0:3, :], bk.rearrange("(j p) o -> j (p o)", p=P))
-        nc.scalar.dma_start(bias_rows[3:6, :], bv.rearrange("(j p) o -> j (p o)", p=P))
-        identity = held.tile([OUT_BLOCKS, OUT_BLOCKS], F32, name="identity")
-        make_identity(nc, identity[:])
-        bias_bank = psum.tile([P, HALF], F32, name="bias_bank", tag="bank")
-        nc.tensor.matmul(bias_bank[:, 0:OUT_BLOCKS], bias_rows[:], identity[:], start=True, stop=True)
-        bias = held.tile([P, OUT_BLOCKS], F32, name="bias")
-        nc.vector.tensor_copy(bias[:], bias_bank[:, 0:OUT_BLOCKS])
-
         def load_given(kb, h):
             slot, kind = divmod(kb, SLOT_BLOCKS)
             first = slot * NODES + h * HALF
@@ -68,6 +57,10 @@ def tile_tgnlayergraphattentionembedding_kernel(
                     nc.sync.dma_start(table[b][:], features[b * P : (b + 1) * P, :])
         for kb in given_blocks:
             load_given(kb, 1)
+        bias = [held.tile([P, Q // P], F32, name=f"bias{v}") for v in range(2)]
+        with nc.allow_non_contiguous_dma(reason="one bias element to a partition: 4-byte pieces"):
+            nc.sync.dma_start(bias[0][:], bk.rearrange("(i p) o -> p (i o)", p=P))
+            nc.sync.dma_start(bias[1][:], bv.rearrange("(i p) o -> p (i o)", p=P))
 
         for h in range(HALVES):
             for slot in range(SLOTS):
@@ -80,7 +73,8 @@ def tile_tgnlayergraphattentionembedding_kernel(
 
         def finish(bank, j, h):
             staged = ring.tile([P, HALF], F32, name="staged")
-            nc.vector.tensor_scalar_add(staged[:], bank[:], bias[:, j : j + 1])
+            v, i = divmod(j, Q // P)
+            nc.vector.tensor_scalar_add(staged[:], bank[:], bias[v][:, i : i + 1])
             nc.sync.dma_start(out[j * P : (j + 1) * P, h * HALF : (h + 1) * HALF], staged[:])
 
         banks = [psum.tile([P, HALF], F32, name=f"bank{j}", tag="bank") for j in range(OUT_BLOCKS)]

@@ -15,6 +15,7 @@ SLOT_BLOCKS = 4
 K_BLOCKS = SLOTS * SLOT_BLOCKS
 Q = 384
 OUT_BLOCKS = 2 * Q // P
+WARM_UPS = 5
 
 FLOPS = 2 * (2 * Q) * (K_BLOCKS * P) * NODES
 
@@ -40,6 +41,12 @@ def tile_tgnlayergraphattentionembedding_kernel(
         given_blocks = [kb for kb in range(K_BLOCKS) if kb % SLOT_BLOCKS in given]
         neigh_blocks = [kb for kb in range(K_BLOCKS) if kb % SLOT_BLOCKS not in given]
         k_order = given_blocks + neigh_blocks
+
+        zeros = held.tile([P, HALF], BF16, name="zeros")
+        nc.vector.memset(zeros[:], 0.0)
+        unread = psum.tile([P, HALF], F32, name="unread", tag="bank")
+        for turn in range(WARM_UPS):
+            nc.tensor.matmul(unread[:], zeros[:, 0:P], zeros[:], start=True, stop=True)
 
         def load_given(kb, h):
             slot, kind = divmod(kb, SLOT_BLOCKS)

@@ -15,6 +15,7 @@ SLOT_BLOCKS = 4
 K_BLOCKS = SLOTS * SLOT_BLOCKS
 Q = 384
 OUT_BLOCKS = 2 * Q // P
+LAST_WIDTH = 128
 WARM_UPS = 5
 
 FLOPS = 2 * (2 * Q) * (K_BLOCKS * P) * NODES
@@ -78,11 +79,11 @@ def tile_tgnlayergraphattentionembedding_kernel(
                     nc.scalar.activation(picked[:], table[b][:].indirect(piece), COPY)
                     nc.vector.tensor_copy(agg[slot * SLOT_BLOCKS + b][h][:], picked[:])
 
-        def finish(bank, j, h):
+        def finish(bank, j, first, width):
             staged = ring.tile([P, HALF], F32, name="staged")
             v, i = divmod(j, Q // P)
-            nc.vector.tensor_scalar_add(staged[:], bank[:], bias[v][:, i : i + 1])
-            nc.sync.dma_start(out[j * P : (j + 1) * P, h * HALF : (h + 1) * HALF], staged[:])
+            nc.vector.tensor_scalar_add(staged[:, 0:width], bank[:, 0:width], bias[v][:, i : i + 1])
+            nc.sync.dma_start(out[j * P : (j + 1) * P, first : first + width], staged[:, 0:width])
 
         banks = [psum.tile([P, HALF], F32, name=f"bank{j}", tag="bank") for j in range(OUT_BLOCKS)]
         for place, kb in enumerate(k_order):
@@ -95,16 +96,18 @@ def tile_tgnlayergraphattentionembedding_kernel(
                     stop=place == K_BLOCKS - 1,
                 )
         for j in range(OUT_BLOCKS):
-            finish(banks[j], j, 0)
+            finish(banks[j], j, 0, HALF)
 
         for j in range(OUT_BLOCKS):
-            bank = psum.tile([P, HALF], F32, name="bank", tag="bank")
-            for place, kb in enumerate(k_order):
-                nc.tensor.matmul(
-                    bank[:],
-                    weights[kb][:, j * P : (j + 1) * P],
-                    agg[kb][1][:],
-                    start=place == 0,
-                    stop=place == K_BLOCKS - 1,
-                )
-            finish(bank, j, 1)
+            width = LAST_WIDTH if j == OUT_BLOCKS - 1 else HALF
+            for first in range(0, HALF, width):
+                bank = psum.tile([P, HALF], F32, name="bank", tag="bank")
+                for place, kb in enumerate(k_order):
+                    nc.tensor.matmul(
+                        bank[:, 0:width],
+                        weights[kb][:, j * P : (j + 1) * P],
+                        agg[kb][1][:, first : first + width],
+                        start=place == 0,
+                        stop=place == K_BLOCKS - 1,
+                    )
+                finish(bank, j, HALF + first, width)

@@ -16,6 +16,7 @@ K_BLOCKS = SLOTS * SLOT_BLOCKS
 Q = 384
 OUT_BLOCKS = 2 * Q // P
 LAST_WIDTH = 128
+TABLE_PLACE = 5
 WARM_UPS = 5
 
 FLOPS = 2 * (2 * Q) * (K_BLOCKS * P) * NODES
@@ -59,7 +60,7 @@ def tile_tgnlayergraphattentionembedding_kernel(
             nc.sync.dma_start(weights[kb][:, Q : 2 * Q], wv[kb * P : (kb + 1) * P, :])
             if kb in given_blocks:
                 load_given(kb, 0)
-            if place == 2:
+            if place == TABLE_PLACE:
                 nc.sync.dma_start(offsets[:], offs)
                 for b in range(TABLE_BLOCKS):
                     nc.sync.dma_start(table[b][:], features[b * P : (b + 1) * P, :])

@@ -17,7 +17,7 @@ Q = 384
 OUT_BLOCKS = 2 * Q // P
 LAST_WIDTH = 128
 TABLE_PLACE = 5
-WARM_UPS = 5
+WARM_UPS = 3
 
 FLOPS = 2 * (2 * Q) * (K_BLOCKS * P) * NODES
 

@@ -56,10 +56,10 @@ def tile_tgnlayergraphattentionembedding_kernel(
             nc.sync.dma_start(agg[kb][h][:], given[kind][:, first : first + HALF])
 
         for place, kb in enumerate(k_order):
-            nc.sync.dma_start(weights[kb][:, 0:Q], wk[kb * P : (kb + 1) * P, :])
-            nc.sync.dma_start(weights[kb][:, Q : 2 * Q], wv[kb * P : (kb + 1) * P, :])
             if kb in given_blocks:
                 load_given(kb, 0)
+            nc.sync.dma_start(weights[kb][:, 0:Q], wk[kb * P : (kb + 1) * P, :])
+            nc.sync.dma_start(weights[kb][:, Q : 2 * Q], wv[kb * P : (kb + 1) * P, :])
             if place == TABLE_PLACE:
                 nc.sync.dma_start(offsets[:], offs)
                 for b in range(TABLE_BLOCKS):

@@ -16,7 +16,7 @@ K_BLOCKS = SLOTS * SLOT_BLOCKS
 Q = 384
 OUT_BLOCKS = 2 * Q // P
 LAST_WIDTH = 128
-TABLE_PLACE = 5
+TABLE_PLACE = 3
 WARM_UPS = 3
 
 FLOPS = 2 * (2 * Q) * (K_BLOCKS * P) * NODES

@@ -16,7 +16,7 @@ K_BLOCKS = SLOTS * SLOT_BLOCKS
 Q = 384
 OUT_BLOCKS = 2 * Q // P
 LAST_WIDTH = 128
-TABLE_PLACE = 3
+TABLE_PLACE = 4
 WARM_UPS = 3
 
 FLOPS = 2 * (2 * Q) * (K_BLOCKS * P) * NODES

@@ -17,7 +17,7 @@ Q = 384
 OUT_BLOCKS = 2 * Q // P
 LAST_WIDTH = 128
 TABLE_PLACE = 4
-WARM_UPS = 3
+WARM_UPS = 12
 
 FLOPS = 2 * (2 * Q) * (K_BLOCKS * P) * NODES
 
@@ -44,11 +44,11 @@ def tile_tgnlayergraphattentionembedding_kernel(
         neigh_blocks = [kb for kb in range(K_BLOCKS) if kb % SLOT_BLOCKS not in given]
         k_order = given_blocks + neigh_blocks
 
-        zeros = held.tile([P, HALF], BF16, name="zeros")
+        zeros = held.tile([P, P], BF16, name="zeros")
         nc.vector.memset(zeros[:], 0.0)
         unread = psum.tile([P, HALF], F32, name="unread", tag="bank")
         for turn in range(WARM_UPS):
-            nc.tensor.matmul(unread[:], zeros[:, 0:P], zeros[:], start=True, stop=True)
+            nc.tensor.matmul(unread[:, 0:P], zeros[:], zeros[:], start=True, stop=True)
 
         def load_given(kb, h):
             slot, kind = divmod(kb, SLOT_BLOCKS)

import concourse.mybir as mybir

F32 = mybir.dt.float32
BF16 = mybir.dt.bfloat16
U16 = mybir.dt.uint16
COPY = mybir.ActivationFunctionType.Copy

P = 128
NODES = 1024
SLOTS = 4
HALF = 512
HALVES = NODES // HALF
TABLE_BLOCKS = 2
SLOT_BLOCKS = 4
K_BLOCKS = SLOTS * SLOT_BLOCKS
Q = 384
OUT_BLOCKS = 2 * Q // P
LAST_WIDTH = 128
TABLE_PLACE = 4
WARM_UPS = 12

FLOPS = 2 * (2 * Q) * (K_BLOCKS * P) * NODES


def tile_tgnlayergraphattentionembedding_kernel(
    tc, features, edge_feats, time_feats, wk, bk, wv, bv, offs, out
):
    nc = tc.nc
    with (
        tc.tile_pool(name="held", bufs=1) as held,
        tc.tile_pool(name="ring", bufs=4) as ring,
        tc.psum_pool(name="psum", bufs=8) as psum,
    ):
        offsets = held.tile([P, SLOTS * NODES // 16], U16, name="offsets")
        table = [held.tile([P, NODES], F32, name=f"table{b}") for b in range(TABLE_BLOCKS)]
        weights = [held.tile([P, 2 * Q], BF16, name=f"weights{kb}") for kb in range(K_BLOCKS)]
        agg = [
            [held.tile([P, HALF], BF16, name=f"agg{kb}_{h}") for h in range(HALVES)]
            for kb in range(K_BLOCKS)
        ]

        given = {2: edge_feats, 3: time_feats}
        given_blocks = [kb for kb in range(K_BLOCKS) if kb % SLOT_BLOCKS in given]
        neigh_blocks = [kb for kb in range(K_BLOCKS) if kb % SLOT_BLOCKS not in given]
        k_order = given_blocks + neigh_blocks

        zeros = held.tile([P, P], BF16, name="zeros")
        nc.vector.memset(zeros[:], 0.0)
        unread = psum.tile([P, HALF], F32, name="unread", tag="bank")
        for turn in range(WARM_UPS):
            nc.tensor.matmul(unread[:, 0:P], zeros[:], zeros[:], start=True, stop=True)

        def load_given(kb, h):
            slot, kind = divmod(kb, SLOT_BLOCKS)
            first = slot * NODES + h * HALF
            nc.sync.dma_start(agg[kb][h][:], given[kind][:, first : first + HALF])

        for place, kb in enumerate(k_order):
            if kb in given_blocks:
                load_given(kb, 0)
            nc.sync.dma_start(weights[kb][:, 0:Q], wk[kb * P : (kb + 1) * P, :])
            nc.sync.dma_start(weights[kb][:, Q : 2 * Q], wv[kb * P : (kb + 1) * P, :])
            if place == TABLE_PLACE:
                nc.sync.dma_start(offsets[:], offs)
                for b in range(TABLE_BLOCKS):
                    nc.sync.dma_start(table[b][:], features[b * P : (b + 1) * P, :])
        for kb in given_blocks:
            load_given(kb, 1)
        bias = [held.tile([P, Q // P], F32, name=f"bias{v}") for v in range(2)]
        with nc.allow_non_contiguous_dma(reason="one bias element to a partition: 4-byte pieces"):
            nc.sync.dma_start(bias[0][:], bk.rearrange("(i p) o -> p (i o)", p=P))
            nc.sync.dma_start(bias[1][:], bv.rearrange("(i p) o -> p (i o)", p=P))

        for h in range(HALVES):
            for slot in range(SLOTS):
                first = (slot * NODES + h * HALF) // 16
                piece = offsets[:, first : first + HALF // 16]
                for b in range(TABLE_BLOCKS):
                    picked = ring.tile([P, HALF], F32, name="picked")
                    nc.scalar.activation(picked[:], table[b][:].indirect(piece), COPY)
                    nc.vector.tensor_copy(agg[slot * SLOT_BLOCKS + b][h][:], picked[:])

        def finish(bank, j, first, width):
            staged = ring.tile([P, HALF], F32, name="staged")
            v, i = divmod(j, Q // P)
            nc.vector.tensor_scalar_add(staged[:, 0:width], bank[:, 0:width], bias[v][:, i : i + 1])
            nc.sync.dma_start(out[j * P : (j + 1) * P, first : first + width], staged[:, 0:width])

        banks = [psum.tile([P, HALF], F32, name=f"bank{j}", tag="bank") for j in range(OUT_BLOCKS)]
        for place, kb in enumerate(k_order):
            for j in range(OUT_BLOCKS):
                nc.tensor.matmul(
                    banks[j][:],
                    weights[kb][:, j * P : (j + 1) * P],
                    agg[kb][0][:],
                    start=place == 0,
                    stop=place == K_BLOCKS - 1,
                )
        for j in range(OUT_BLOCKS):
            finish(banks[j], j, 0, HALF)

        for j in range(OUT_BLOCKS):
            width = LAST_WIDTH if j == OUT_BLOCKS - 1 else HALF
            for first in range(0, HALF, width):
                bank = psum.tile([P, HALF], F32, name="bank", tag="bank")
                for place, kb in enumerate(k_order):
                    nc.tensor.matmul(
                        bank[:, 0:width],
                        weights[kb][:, j * P : (j + 1) * P],
                        agg[kb][1][:, first : first + width],
                        start=place == 0,
                        stop=place == K_BLOCKS - 1,
                    )
                finish(bank, j, HALF + first, width)
